import numpy as np
import ml_dtypes


def mxq(x, axis, fmt="e4m3"):
    dtype, down = {"e4m3": (ml_dtypes.float8_e4m3fn, 7), "e5m2": (ml_dtypes.float8_e5m2, 14)}[fmt]
    v = np.moveaxis(np.asarray(x, np.float32).astype(ml_dtypes.bfloat16).astype(np.float64), axis, -1)
    blocks = v.reshape(v.shape[:-1] + (-1, 32))
    amax = np.abs(blocks).max(-1, keepdims=True)
    byte = np.maximum(np.where(amax > 0, np.frexp(amax)[1] - 1 + 127, 0) - down, 1)
    scale = np.exp2(byte - 127.0)
    codes = (blocks / scale).astype(np.float32).astype(dtype).astype(np.float64)
    return np.moveaxis((codes * scale).reshape(v.shape), -1, axis)


WIDE = False


def mx_kscale(k):
    if not WIDE:
        return np.ones(k)
    levels = np.array([10, -10, 5, -5, 0])
    a = np.random.permutation(np.resize(levels, k // 512 * 4)).reshape(k // 512, 4)
    idx = np.arange(k)
    return np.exp2(a[idx // 512, idx % 128 // 32])


BF16 = ml_dtypes.bfloat16


def bf(x):
    return np.asarray(x, np.float32).astype(BF16)


def f64(x):
    return np.asarray(x).astype(np.float64)


M, N, E, P, S, B, KT = 512, 512, 4, 32, 17, 4096, 2


def setup_inputs():
    s = mx_kscale(M)
    return {
        "z": bf(np.random.standard_normal((M, B)) * s[:, None]),
        "mlp_out": bf(np.random.standard_normal((B, E)) * 0.65),
        "t2": bf(0.5 + 0.1 * np.random.random_sample(1)),
        "A": bf(np.random.standard_normal((E, M)) * 0.5 / s),
        "W": bf(np.random.standard_normal((E, M, M)) / np.sqrt(M) / s),
        "h": bf(np.random.standard_normal((E, M)) * 0.1),
    }


def reference(z, mlp_out, t2, A, W, h):
    z = f64(z)
    lg = -f64(mlp_out).T / f64(t2)[0]
    ex = np.exp(lg - lg.max(axis=0, keepdims=True))
    w_exp = ex / ex.sum(axis=0, keepdims=True)
    zcat = np.concatenate([z[:-P], np.maximum(z[-P:], 0.0)], axis=0)
    Az = f64(A)[:, :, None] * z[None, :, :]
    Wz = mxq(f64(W), 2, "e4m3") @ mxq(zcat, 0, "e4m3")
    expert_out = Az + Wz + f64(h)[:, :, None]
    return np.sum(expert_out * w_exp[:, None, :], axis=0)

@@ -1,0 +1,246 @@
+from contextlib import ExitStack
+
+import concourse.mybir as mybir
+from concourse.masks import make_identity
+
+F32 = mybir.dt.float32
+BF16 = mybir.dt.bfloat16
+I32 = mybir.dt.int32
+U32 = mybir.dt.uint32
+U8 = mybir.dt.uint8
+FP8X4 = mybir.dt.float8_e4m3fn_x4
+ALU = mybir.AluOpType
+ACT = mybir.ActivationFunctionType
+AX = mybir.AxisListType
+
+P = 128
+M = 512
+B = 4096
+E = 4
+NT = B // P
+GW = 512
+NG = B // GW
+TPG = GW // P
+MT = M // P
+POOL_TILES = [0, 2, 2, 2, 2, 2, 2, 2]
+
+FLOPS = 2 * E * M * M * B
+
+
+def tile_dynamix_pb_t_kernel(tc, z, mlp_out, t2, A, W, h, out):
+    nc = tc.nc
+    with ExitStack() as ctx:
+        ctx.enter_context(tc.manual_schedule())
+        keep = ctx.enter_context(tc.tile_pool(name="keep", bufs=1))
+        stage = ctx.enter_context(tc.tile_pool(name="stage", bufs=2))
+        fields = ctx.enter_context(tc.tile_pool(name="fields", bufs=8))
+        outs = ctx.enter_context(tc.tile_pool(name="outs", bufs=6))
+        pp = ctx.enter_context(tc.psum_pool(name="pp", bufs=4))
+        ps2 = ctx.enter_context(tc.psum_pool(name="ps2", bufs=2))
+
+        z_raw = keep.tile([P, 5, B], BF16, name="z_raw")
+        zq = keep.tile([P, B], U32, name="zq", align_bytes=64)
+        zs = keep.tile([P, B], U8, name="zs", align_bytes=64)
+        w_raw = keep.tile([P, E * MT, M], BF16, name="w_raw")
+        wq = keep.tile([P, E, M], U32, name="wq", align_bytes=64)
+        ws = keep.tile([P, E, M], U8, name="ws", align_bytes=64)
+        gate_rows = keep.tile([P, B], BF16, name="gate_rows")
+        gate_pad = keep.tile([P, NT, P], BF16, name="gate_pad")
+        a_pad = keep.tile([P, M], BF16, name="a_pad")
+        h_pad = keep.tile([P, M], BF16, name="h_pad")
+        h_bc = keep.tile([P, E, M], BF16, name="h_bc")
+        dh = keep.tile([P, E - 1, M], F32, name="dh")
+        h_col = keep.tile([P, MT], F32, name="h_col")
+        ident_f = keep.tile([P, P], F32, name="ident_f")
+        ident_b = keep.tile([P, P], BF16, name="ident_b")
+        warm = keep.tile([P, 1], F32, name="warm")
+        ml = keep.tile([P, NT, E], BF16, name="ml")
+        t2b = keep.tile([P, 1], BF16, name="t2b")
+        t2f = keep.tile([P, 1], F32, name="t2f")
+        rinv = keep.tile([P, 1], F32, name="rinv")
+        lg = keep.tile([P, NT, E], F32, name="lg")
+        mx = keep.tile([P, NT], F32, name="mx")
+        ex = keep.tile([P, NT, E], F32, name="ex")
+        sm = keep.tile([P, NT], F32, name="sm")
+        rs = keep.tile([P, NT], F32, name="rs")
+        gate = keep.tile([P, NT, E], F32, name="gate")
+        g3m1 = keep.tile([P, NT], F32, name="g3m1")
+
+        z_view = z.rearrange("(t p) b -> p t b", p=P)
+
+        def load_z(g):
+            gs = slice(GW * g, GW * (g + 1))
+            nc.sync.dma_start(out=z_raw[:, 1:5, gs], in_=z_view[:, :, gs])
+
+        with nc.allow_non_contiguous_dma(reason="gate logits: 8-byte rows"):
+            nc.scalar.dma_start(out=t2b[:], in_=t2.partition_broadcast(P))
+            nc.scalar.dma_start(out=ml[:], in_=mlp_out.rearrange("(t p) e -> p t e", p=P))
+        load_z(0)
+        nc.sync.dma_start(out=z_raw[:, 0, 0:GW], in_=z_view[:, 3, 0:GW])
+        for e in range(E):
+            nc.sync.dma_start(
+                out=w_raw[:, MT * e:MT * (e + 1), :],
+                in_=W[e].rearrange("(mt p) k -> p mt k", p=P),
+            )
+        load_z(1)
+        nc.sync.dma_start(out=z_raw[:, 0, GW:B], in_=z_view[:, 3, GW:B])
+        nc.sync.dma_start(out=h_bc[:].rearrange("p e m -> p (e m)"),
+                          in_=h.rearrange("e m -> (e m)").partition_broadcast(P))
+        for g in range(2, NG):
+            load_z(g)
+
+        nc.vector.memset(warm[:], 0.0)
+        nc.scalar.activation(out=warm[:], in_=warm[:], func=ACT.Exp)
+        nc.vector.memset(a_pad[:].bitcast(I32), 0)
+        nc.vector.memset(h_pad[:].bitcast(I32), 0)
+        nc.vector.memset(gate_pad[:].rearrange("p t c -> p (t c)").bitcast(I32), 0)
+        make_identity(nc, ident_b[:])
+        make_identity(nc, ident_f[:])
+        for part in range(2):
+            nc.gpsimd.dma_start(out=a_pad[E * part:E * (part + 1), :], in_=A)
+            nc.gpsimd.dma_start(out=h_pad[E * part:E * part + 3, :], in_=h[0:3, :])
+            nc.gpsimd.dma_start(out=h_pad[8 + part:9 + part, :], in_=h[3:4, :])
+
+        nc.vector.tensor_copy(out=t2f[:], in_=t2b[:])
+        nc.vector.reciprocal(out=rinv[:], in_=t2f[:])
+        nc.vector.tensor_scalar(out=lg[:], in0=ml[:], scalar1=rinv[:, 0:1], scalar2=-1.0,
+                                op0=ALU.mult, op1=ALU.mult)
+        nc.vector.tensor_reduce(out=mx[:], in_=lg[:], axis=AX.X, op=ALU.max)
+        nc.vector.tensor_tensor(out=lg[:], in0=lg[:], in1=mx[:].unsqueeze(2).to_broadcast([P, NT, E]),
+                                op=ALU.subtract)
+        nc.scalar.activation(out=ex[:], in_=lg[:], func=ACT.Exp)
+        nc.vector.tensor_reduce(out=sm[:], in_=ex[:], axis=AX.X, op=ALU.add)
+        nc.vector.reciprocal(out=rs[:], in_=sm[:])
+        nc.vector.tensor_tensor(out=gate[:], in0=ex[:], in1=rs[:].unsqueeze(2).to_broadcast([P, NT, E]),
+                                op=ALU.mult)
+
+        z_grouped = {}
+
+        def regroup_z(g):
+            gs = slice(GW * g, GW * (g + 1))
+            nc.scalar.activation(out=z_raw[96:128, 0, gs], in_=z_raw[96:128, 0, gs], func=ACT.Relu)
+            zg = stage.tile([P, GW, 4], BF16, tag="zg", align_bytes=64)
+            nc.scalar.copy(
+                out=zg[:].rearrange("p (c i) t -> p c t i", i=4),
+                in_=z_raw[:, 0:4, gs].rearrange("p t (c i) -> p c t i", i=4),
+            )
+            z_grouped[g] = zg
+
+        def quantise_z(g):
+            gs = slice(GW * g, GW * (g + 1))
+            nc.vector.quantize_mx(out=zq[:, gs].bitcast(FP8X4), scales=zs[:, gs],
+                                  in_=z_grouped[g][:].rearrange("p b t -> p (b t)"))
+
+        regroup_z(0)
+        quantise_z(0)
+
+        for e in range(E):
+            wg = stage.tile([P, M, 4], BF16, tag="wg", align_bytes=64)
+            for half in range(2):
+                xt = pp.tile([P, 8, P], BF16, tag="P")
+                for a in range(2):
+                    mt = 2 * half + a
+                    for j in range(4):
+                        t = (j + 3) % 4
+                        nc.tensor.transpose(xt[:, 4 * a + j, :], w_raw[:, MT * e + mt, P * t:P * (t + 1)],
+                                            ident_b[:])
+                dst = wg[:, 256 * half:256 * (half + 1), :].rearrange("p (a r) j -> p a r j", a=2)
+                src = xt[:].rearrange("p (a j) r -> p a r j", a=2)
+                if half == 0:
+                    nc.vector.tensor_copy(out=dst, in_=src)
+                else:
+                    nc.scalar.copy(out=dst, in_=src)
+            nc.vector.quantize_mx(out=wq[:, e, :].bitcast(FP8X4), scales=ws[:, e, :],
+                                  in_=wg[:].rearrange("p m j -> p (m j)"))
+        regroup_z(1)
+
+        for e in range(E - 1):
+            nc.gpsimd.tensor_tensor(out=dh[:, e, :], in0=h_bc[:, e, :], in1=h_bc[:, 3, :], op=ALU.subtract)
+        pool_h = {}
+        for g in range(NG):
+            for i in range(TPG - POOL_TILES[g], TPG):
+                tb = TPG * g + i
+                gh = keep.tile([P, M], F32, name="gh%d" % tb)
+                nc.gpsimd.tensor_scalar(out=gh[:], in0=dh[:, 0, :], scalar1=gate[:, tb, 0:1], scalar2=0.0,
+                                        op0=ALU.mult, op1=ALU.add)
+                for e in range(1, E - 1):
+                    tm = stage.tile([P, M], F32, tag="tm")
+                    nc.gpsimd.tensor_scalar(out=tm[:], in0=dh[:, e, :], scalar1=gate[:, tb, e:e + 1], scalar2=0.0,
+                                            op0=ALU.mult, op1=ALU.add)
+                    nc.gpsimd.tensor_tensor(out=gh[:], in0=gh[:], in1=tm[:], op=ALU.add)
+                pool_h[tb] = gh
+
+        group_fields = {}
+
+        def experts(g):
+            rows = []
+            for i in range(TPG):
+                tb = TPG * g + i
+                bs = slice(P * tb, P * (tb + 1))
+                acc = []
+                for e in range(E):
+                    pe = pp.tile([P, M], F32, tag="P")
+                    nc.tensor.matmul_mx(out=pe[:], lhsT=zq[:, bs].bitcast(FP8X4), lhsT_scale=zs[:, bs],
+                                        rhs=wq[:, e, :].bitcast(FP8X4), rhs_scale=ws[:, e, :],
+                                        start=True, stop=True)
+                    if e % 2 == 0:
+                        fld = fields.tile([P, M], F32, tag="f%d" % (e // 2))
+                        nc.scalar.activation(out=fld[:], in_=pe[:], func=ACT.Copy, scale=gate[:, tb, e:e + 1])
+                        acc.append(fld)
+                    else:
+                        fld = acc[-1]
+                        nc.vector.scalar_tensor_tensor(out=fld[:], in0=pe[:], scalar=gate[:, tb, e:e + 1],
+                                                       in1=fld[:], op0=ALU.mult, op1=ALU.add)
+                if tb in pool_h:
+                    acc.append(pool_h[tb])
+                rows.append(acc)
+            group_fields[g] = rows
+
+        def finish(g):
+            gs = slice(GW * g, GW * (g + 1))
+            rows = group_fields[g]
+            wide = GW - P * POOL_TILES[g]
+            if g + 2 < NG:
+                regroup_z(g + 2)
+            for mt in range(MT):
+                ms = slice(P * mt, P * (mt + 1))
+                b2 = ps2.tile([P, GW], F32, tag="b2")
+                nc.tensor.matmul(out=b2[:], lhsT=a_pad[:, ms], rhs=gate_rows[:, gs], start=True, stop=True)
+                b1 = ps2.tile([P, GW], F32, tag="b1")
+                nc.tensor.matmul(out=b1[:, 0:wide], lhsT=h_pad[:, ms],
+                                 rhs=gate_rows[:, GW * g:GW * g + wide], start=True, stop=False)
+                todo = [(i, fld) for i in range(TPG) for fld in rows[i]]
+                for n, (i, fld) in enumerate(todo):
+                    nc.tensor.matmul(out=b1[:, P * i:P * (i + 1)], lhsT=fld[:, ms], rhs=ident_f[:],
+                                     is_transpose=True, start=False, stop=(n == len(todo) - 1))
+                xs = outs.tile([P, GW], F32, tag="xs")
+                nc.vector.tensor_tensor(out=xs[:], in0=b2[:], in1=z_raw[:, 1 + mt, gs], op=ALU.mult)
+                nc.vector.scalar_tensor_tensor(out=xs[:], in0=b1[:], scalar=h_col[:, mt:mt + 1], in1=xs[:],
+                                               op0=ALU.add, op1=ALU.add)
+                nc.sync.dma_start(out=out[ms, gs], in_=xs[:])
+            if g + 2 < NG:
+                quantise_z(g + 2)
+
+        experts(0)
+
+        nc.vector.tensor_copy(out=gate_pad[:, :, 0:E], in_=gate[:])
+        nc.vector.tensor_tensor(out=gate_pad[:, :, E:2 * E], in0=gate[:], in1=gate_pad[:, :, 0:E],
+                                op=ALU.subtract)
+        nc.vector.tensor_scalar_add(out=g3m1[:], in0=gate[:, :, 3], scalar1=-1.0)
+        nc.vector.tensor_copy(out=gate_pad[:, :, 8], in_=g3m1[:])
+        nc.vector.tensor_tensor(out=gate_pad[:, :, 9], in0=g3m1[:], in1=gate_pad[:, :, 8], op=ALU.subtract)
+        for q in range(4):
+            wt = ps2.tile([P, 8, P], BF16, tag="b1")
+            for i in range(8):
+                nc.tensor.transpose(wt[:, i, :], gate_pad[:, 8 * q + i, :], ident_b[:])
+            nc.scalar.copy(out=gate_rows[:, 1024 * q:1024 * (q + 1)], in_=wt[:].rearrange("p t c -> p (t c)"))
+        ht = ps2.tile([P, MT, P], BF16, tag="b2")
+        for mt in range(MT):
+            nc.tensor.transpose(ht[:, mt, :], h_pad[:, P * mt:P * (mt + 1)], ident_b[:])
+        nc.vector.tensor_copy(out=h_col[:], in_=ht[:, :, 8])
+        quantise_z(1)
+
+        for g in range(NG):
+            if g + 1 < NG:
+                experts(g + 1)
+            finish(g)

@@ -22,7 +22,7 @@ GW = 512
 NG = B // GW
 TPG = GW // P
 MT = M // P
-POOL_TILES = [0, 2, 2, 2, 2, 2, 2, 2]
+OFF_TILES = [2, 2, 2, 2, 2, 2, 2, 0]
 
 FLOPS = 2 * E * M * M * B
 
@@ -30,10 +30,10 @@ FLOPS = 2 * E * M * M * B
 def tile_dynamix_pb_t_kernel(tc, z, mlp_out, t2, A, W, h, out):
     nc = tc.nc
     with ExitStack() as ctx:
-        ctx.enter_context(tc.manual_schedule())
         keep = ctx.enter_context(tc.tile_pool(name="keep", bufs=1))
         stage = ctx.enter_context(tc.tile_pool(name="stage", bufs=2))
         fields = ctx.enter_context(tc.tile_pool(name="fields", bufs=8))
+        hfields = ctx.enter_context(tc.tile_pool(name="hfields", bufs=4))
         outs = ctx.enter_context(tc.tile_pool(name="outs", bufs=6))
         pp = ctx.enter_context(tc.psum_pool(name="pp", bufs=4))
         ps2 = ctx.enter_context(tc.psum_pool(name="ps2", bufs=2))
@@ -84,10 +84,10 @@ def tile_dynamix_pb_t_kernel(tc, z, mlp_out, t2, A, W, h, out):
             )
         load_z(1)
         nc.sync.dma_start(out=z_raw[:, 0, GW:B], in_=z_view[:, 3, GW:B])
-        nc.sync.dma_start(out=h_bc[:].rearrange("p e m -> p (e m)"),
-                          in_=h.rearrange("e m -> (e m)").partition_broadcast(P))
         for g in range(2, NG):
             load_z(g)
+        nc.sync.dma_start(out=h_bc[:].rearrange("p e m -> p (e m)"),
+                          in_=h.rearrange("e m -> (e m)").partition_broadcast(P))
 
         nc.vector.memset(warm[:], 0.0)
         nc.scalar.activation(out=warm[:], in_=warm[:], func=ACT.Exp)
@@ -101,24 +101,14 @@ def tile_dynamix_pb_t_kernel(tc, z, mlp_out, t2, A, W, h, out):
             nc.gpsimd.dma_start(out=h_pad[E * part:E * part + 3, :], in_=h[0:3, :])
             nc.gpsimd.dma_start(out=h_pad[8 + part:9 + part, :], in_=h[3:4, :])
 
-        nc.vector.tensor_copy(out=t2f[:], in_=t2b[:])
-        nc.vector.reciprocal(out=rinv[:], in_=t2f[:])
-        nc.vector.tensor_scalar(out=lg[:], in0=ml[:], scalar1=rinv[:, 0:1], scalar2=-1.0,
-                                op0=ALU.mult, op1=ALU.mult)
-        nc.vector.tensor_reduce(out=mx[:], in_=lg[:], axis=AX.X, op=ALU.max)
-        nc.vector.tensor_tensor(out=lg[:], in0=lg[:], in1=mx[:].unsqueeze(2).to_broadcast([P, NT, E]),
-                                op=ALU.subtract)
-        nc.scalar.activation(out=ex[:], in_=lg[:], func=ACT.Exp)
-        nc.vector.tensor_reduce(out=sm[:], in_=ex[:], axis=AX.X, op=ALU.add)
-        nc.vector.reciprocal(out=rs[:], in_=sm[:])
-        nc.vector.tensor_tensor(out=gate[:], in0=ex[:], in1=rs[:].unsqueeze(2).to_broadcast([P, NT, E]),
-                                op=ALU.mult)
-
         z_grouped = {}
+
+        def relu_z(g):
+            gs = slice(GW * g, GW * (g + 1))
+            nc.vector.tensor_scalar_max(out=z_raw[96:128, 0, gs], in0=z_raw[96:128, 0, gs], scalar1=0.0)
 
         def regroup_z(g):
             gs = slice(GW * g, GW * (g + 1))
-            nc.scalar.activation(out=z_raw[96:128, 0, gs], in_=z_raw[96:128, 0, gs], func=ACT.Relu)
             zg = stage.tile([P, GW, 4], BF16, tag="zg", align_bytes=64)
             nc.scalar.copy(
                 out=zg[:].rearrange("p (c i) t -> p c t i", i=4),
@@ -131,7 +121,20 @@ def tile_dynamix_pb_t_kernel(tc, z, mlp_out, t2, A, W, h, out):
             nc.vector.quantize_mx(out=zq[:, gs].bitcast(FP8X4), scales=zs[:, gs],
                                   in_=z_grouped[g][:].rearrange("p b t -> p (b t)"))
 
+        nc.vector.tensor_copy(out=t2f[:], in_=t2b[:])
+        nc.vector.reciprocal(out=rinv[:], in_=t2f[:])
+        nc.vector.tensor_scalar(out=lg[:], in0=ml[:], scalar1=rinv[:, 0:1], scalar2=-1.0,
+                                op0=ALU.mult, op1=ALU.mult)
+        nc.vector.tensor_reduce(out=mx[:], in_=lg[:], axis=AX.X, op=ALU.max)
+        nc.vector.tensor_tensor(out=lg[:], in0=lg[:], in1=mx[:].unsqueeze(2).to_broadcast([P, NT, E]),
+                                op=ALU.subtract)
+        nc.scalar.activation(out=ex[:], in_=lg[:], func=ACT.Exp)
+        relu_z(0)
         regroup_z(0)
+        nc.vector.tensor_reduce(out=sm[:], in_=ex[:], axis=AX.X, op=ALU.add)
+        nc.vector.reciprocal(out=rs[:], in_=sm[:])
+        nc.vector.tensor_tensor(out=gate[:], in0=ex[:], in1=rs[:].unsqueeze(2).to_broadcast([P, NT, E]),
+                                op=ALU.mult)
         quantise_z(0)
 
         for e in range(E):
@@ -152,23 +155,28 @@ def tile_dynamix_pb_t_kernel(tc, z, mlp_out, t2, A, W, h, out):
                     nc.scalar.copy(out=dst, in_=src)
             nc.vector.quantize_mx(out=wq[:, e, :].bitcast(FP8X4), scales=ws[:, e, :],
                                   in_=wg[:].rearrange("p m j -> p (m j)"))
+        relu_z(1)
+        relu_z(2)
         regroup_z(1)
 
-        for e in range(E - 1):
-            nc.gpsimd.tensor_tensor(out=dh[:, e, :], in0=h_bc[:, e, :], in1=h_bc[:, 3, :], op=ALU.subtract)
-        pool_h = {}
-        for g in range(NG):
-            for i in range(TPG - POOL_TILES[g], TPG):
-                tb = TPG * g + i
-                gh = keep.tile([P, M], F32, name="gh%d" % tb)
-                nc.gpsimd.tensor_scalar(out=gh[:], in0=dh[:, 0, :], scalar1=gate[:, tb, 0:1], scalar2=0.0,
-                                        op0=ALU.mult, op1=ALU.add)
-                for e in range(1, E - 1):
-                    tm = stage.tile([P, M], F32, tag="tm")
-                    nc.gpsimd.tensor_scalar(out=tm[:], in0=dh[:, e, :], scalar1=gate[:, tb, e:e + 1], scalar2=0.0,
-                                            op0=ALU.mult, op1=ALU.add)
-                    nc.gpsimd.tensor_tensor(out=gh[:], in0=gh[:], in1=tm[:], op=ALU.add)
-                pool_h[tb] = gh
+        off_fields = {}
+
+        def off_tiles(g):
+            return [TPG * g + i for i in range(TPG - OFF_TILES[g], TPG)]
+
+        def gate_h_scalar(g):
+            for tb in off_tiles(g):
+                f0 = hfields.tile([P, M], F32, tag="h0")
+                f2 = hfields.tile([P, M], F32, tag="h2")
+                nc.scalar.activation(out=f0[:], in_=dh[:, 0, :], func=ACT.Copy, scale=gate[:, tb, 0:1])
+                nc.scalar.activation(out=f2[:], in_=dh[:, 2, :], func=ACT.Copy, scale=gate[:, tb, 2:3])
+                off_fields[tb] = [f0, f2]
+
+        def gate_h_vector(g):
+            for tb in off_tiles(g):
+                f0 = off_fields[tb][0]
+                nc.vector.scalar_tensor_tensor(out=f0[:], in0=dh[:, 1, :], scalar=gate[:, tb, 1:2], in1=f0[:],
+                                               op0=ALU.mult, op1=ALU.add)
 
         group_fields = {}
 
@@ -191,17 +199,21 @@ def tile_dynamix_pb_t_kernel(tc, z, mlp_out, t2, A, W, h, out):
                         fld = acc[-1]
                         nc.vector.scalar_tensor_tensor(out=fld[:], in0=pe[:], scalar=gate[:, tb, e:e + 1],
                                                        in1=fld[:], op0=ALU.mult, op1=ALU.add)
-                if tb in pool_h:
-                    acc.append(pool_h[tb])
                 rows.append(acc)
             group_fields[g] = rows
 
         def finish(g):
             gs = slice(GW * g, GW * (g + 1))
             rows = group_fields[g]
-            wide = GW - P * POOL_TILES[g]
+            wide = GW - P * OFF_TILES[g]
             if g + 2 < NG:
                 regroup_z(g + 2)
+            if g + 1 < NG:
+                gate_h_scalar(g + 1)
+            todo = []
+            for i in range(TPG):
+                for fld in rows[i] + off_fields.get(TPG * g + i, []):
+                    todo.append((i, fld))
             for mt in range(MT):
                 ms = slice(P * mt, P * (mt + 1))
                 b2 = ps2.tile([P, GW], F32, tag="b2")
@@ -209,7 +221,6 @@ def tile_dynamix_pb_t_kernel(tc, z, mlp_out, t2, A, W, h, out):
                 b1 = ps2.tile([P, GW], F32, tag="b1")
                 nc.tensor.matmul(out=b1[:, 0:wide], lhsT=h_pad[:, ms],
                                  rhs=gate_rows[:, GW * g:GW * g + wide], start=True, stop=False)
-                todo = [(i, fld) for i in range(TPG) for fld in rows[i]]
                 for n, (i, fld) in enumerate(todo):
                     nc.tensor.matmul(out=b1[:, P * i:P * (i + 1)], lhsT=fld[:, ms], rhs=ident_f[:],
                                      is_transpose=True, start=False, stop=(n == len(todo) - 1))
@@ -218,8 +229,12 @@ def tile_dynamix_pb_t_kernel(tc, z, mlp_out, t2, A, W, h, out):
                 nc.vector.scalar_tensor_tensor(out=xs[:], in0=b1[:], scalar=h_col[:, mt:mt + 1], in1=xs[:],
                                                op0=ALU.add, op1=ALU.add)
                 nc.sync.dma_start(out=out[ms, gs], in_=xs[:])
+            if g + 1 < NG:
+                gate_h_vector(g + 1)
             if g + 2 < NG:
                 quantise_z(g + 2)
+            if g + 3 < NG:
+                relu_z(g + 3)
 
         experts(0)
 
@@ -239,6 +254,10 @@ def tile_dynamix_pb_t_kernel(tc, z, mlp_out, t2, A, W, h, out):
             nc.tensor.transpose(ht[:, mt, :], h_pad[:, P * mt:P * (mt + 1)], ident_b[:])
         nc.vector.tensor_copy(out=h_col[:], in_=ht[:, :, 8])
         quantise_z(1)
+        nc.vector.tensor_tensor(out=dh[:], in0=h_bc[:, 0:3, :], in1=h_bc[:, 3:4, :].to_broadcast([P, E - 1, M]),
+                                op=ALU.subtract)
+        gate_h_scalar(0)
+        gate_h_vector(0)
 
         for g in range(NG):
             if g + 1 < NG:

@@ -22,18 +22,27 @@ GW = 512
 NG = B // GW
 TPG = GW // P
 MT = M // P
-OFF_TILES = [2, 2, 2, 2, 2, 2, 2, 0]
+OFF_TILES = [0, 1, 2, 2, 2, 2, 2, 2]
+LAG = 4
+AHEAD_COPY = 3
+AHEAD_QUANT = 2
+FIELD_BUFS = 10
 
 FLOPS = 2 * E * M * M * B
+
+
+def scalar_experts(tb):
+    return [0] if tb < TPG else [0, 2]
 
 
 def tile_dynamix_pb_t_kernel(tc, z, mlp_out, t2, A, W, h, out):
     nc = tc.nc
     with ExitStack() as ctx:
+        ctx.enter_context(tc.manual_schedule())
         keep = ctx.enter_context(tc.tile_pool(name="keep", bufs=1))
         stage = ctx.enter_context(tc.tile_pool(name="stage", bufs=2))
-        fields = ctx.enter_context(tc.tile_pool(name="fields", bufs=8))
-        hfields = ctx.enter_context(tc.tile_pool(name="hfields", bufs=4))
+        zstage = ctx.enter_context(tc.tile_pool(name="zstage", bufs=6))
+        fields = ctx.enter_context(tc.tile_pool(name="fields", bufs=FIELD_BUFS))
         outs = ctx.enter_context(tc.tile_pool(name="outs", bufs=6))
         pp = ctx.enter_context(tc.psum_pool(name="pp", bufs=4))
         ps2 = ctx.enter_context(tc.psum_pool(name="ps2", bufs=2))
@@ -70,24 +79,24 @@ def tile_dynamix_pb_t_kernel(tc, z, mlp_out, t2, A, W, h, out):
 
         def load_z(g):
             gs = slice(GW * g, GW * (g + 1))
+            nc.sync.dma_start(out=z_raw[:, 0, gs], in_=z_view[:, 3, gs])
             nc.sync.dma_start(out=z_raw[:, 1:5, gs], in_=z_view[:, :, gs])
 
         with nc.allow_non_contiguous_dma(reason="gate logits: 8-byte rows"):
             nc.scalar.dma_start(out=t2b[:], in_=t2.partition_broadcast(P))
             nc.scalar.dma_start(out=ml[:], in_=mlp_out.rearrange("(t p) e -> p t e", p=P))
-        load_z(0)
-        nc.sync.dma_start(out=z_raw[:, 0, 0:GW], in_=z_view[:, 3, 0:GW])
         for e in range(E):
             nc.sync.dma_start(
                 out=w_raw[:, MT * e:MT * (e + 1), :],
                 in_=W[e].rearrange("(mt p) k -> p mt k", p=P),
             )
+        load_z(0)
         load_z(1)
-        nc.sync.dma_start(out=z_raw[:, 0, GW:B], in_=z_view[:, 3, GW:B])
-        for g in range(2, NG):
-            load_z(g)
+        load_z(2)
         nc.sync.dma_start(out=h_bc[:].rearrange("p e m -> p (e m)"),
                           in_=h.rearrange("e m -> (e m)").partition_broadcast(P))
+        for g in range(3, NG):
+            load_z(g)
 
         nc.vector.memset(warm[:], 0.0)
         nc.scalar.activation(out=warm[:], in_=warm[:], func=ACT.Exp)
@@ -97,45 +106,53 @@ def tile_dynamix_pb_t_kernel(tc, z, mlp_out, t2, A, W, h, out):
         make_identity(nc, ident_b[:])
         make_identity(nc, ident_f[:])
         for part in range(2):
-            nc.gpsimd.dma_start(out=a_pad[E * part:E * (part + 1), :], in_=A)
-            nc.gpsimd.dma_start(out=h_pad[E * part:E * part + 3, :], in_=h[0:3, :])
-            nc.gpsimd.dma_start(out=h_pad[8 + part:9 + part, :], in_=h[3:4, :])
+            nc.scalar.dma_start(out=a_pad[E * part:E * (part + 1), :], in_=A)
+            nc.scalar.dma_start(out=h_pad[E * part:E * part + 3, :], in_=h[0:3, :])
+            nc.scalar.dma_start(out=h_pad[8 + part:9 + part, :], in_=h[3:4, :])
 
         z_grouped = {}
 
         def relu_z(g):
             gs = slice(GW * g, GW * (g + 1))
-            nc.vector.tensor_scalar_max(out=z_raw[96:128, 0, gs], in0=z_raw[96:128, 0, gs], scalar1=0.0)
+            nc.scalar.activation(out=z_raw[96:128, 0, gs], in_=z_raw[96:128, 0, gs], func=ACT.Relu)
 
-        def regroup_z(g):
-            gs = slice(GW * g, GW * (g + 1))
-            zg = stage.tile([P, GW, 4], BF16, tag="zg", align_bytes=64)
+        def regroup_z(tb):
+            cs = slice(P * tb, P * (tb + 1))
+            zg = zstage.tile([P, P, 4], BF16, tag="zg", align_bytes=64)
             nc.scalar.copy(
                 out=zg[:].rearrange("p (c i) t -> p c t i", i=4),
-                in_=z_raw[:, 0:4, gs].rearrange("p t (c i) -> p c t i", i=4),
+                in_=z_raw[:, 0:4, cs].rearrange("p t (c i) -> p c t i", i=4),
             )
-            z_grouped[g] = zg
+            z_grouped[tb] = zg
 
-        def quantise_z(g):
-            gs = slice(GW * g, GW * (g + 1))
-            nc.vector.quantize_mx(out=zq[:, gs].bitcast(FP8X4), scales=zs[:, gs],
-                                  in_=z_grouped[g][:].rearrange("p b t -> p (b t)"))
+        def quantise_z(tb):
+            cs = slice(P * tb, P * (tb + 1))
+            nc.vector.quantize_mx(out=zq[:, cs].bitcast(FP8X4), scales=zs[:, cs],
+                                  in_=z_grouped[tb][:].rearrange("p b t -> p (b t)"))
 
-        nc.vector.tensor_copy(out=t2f[:], in_=t2b[:])
-        nc.vector.reciprocal(out=rinv[:], in_=t2f[:])
-        nc.vector.tensor_scalar(out=lg[:], in0=ml[:], scalar1=rinv[:, 0:1], scalar2=-1.0,
-                                op0=ALU.mult, op1=ALU.mult)
-        nc.vector.tensor_reduce(out=mx[:], in_=lg[:], axis=AX.X, op=ALU.max)
-        nc.vector.tensor_tensor(out=lg[:], in0=lg[:], in1=mx[:].unsqueeze(2).to_broadcast([P, NT, E]),
-                                op=ALU.subtract)
-        nc.scalar.activation(out=ex[:], in_=lg[:], func=ACT.Exp)
-        relu_z(0)
-        regroup_z(0)
-        nc.vector.tensor_reduce(out=sm[:], in_=ex[:], axis=AX.X, op=ALU.add)
-        nc.vector.reciprocal(out=rs[:], in_=sm[:])
-        nc.vector.tensor_tensor(out=gate[:], in0=ex[:], in1=rs[:].unsqueeze(2).to_broadcast([P, NT, E]),
-                                op=ALU.mult)
-        quantise_z(0)
+        def softmax_first():
+            nc.vector.tensor_copy(out=t2f[:], in_=t2b[:])
+            nc.vector.reciprocal(out=rinv[:], in_=t2f[:])
+            nc.vector.tensor_scalar(out=lg[:], in0=ml[:], scalar1=rinv[:, 0:1], scalar2=-1.0,
+                                    op0=ALU.mult, op1=ALU.mult)
+            nc.vector.tensor_reduce(out=mx[:], in_=lg[:], axis=AX.X, op=ALU.max)
+            nc.vector.tensor_tensor(out=lg[:], in0=lg[:], in1=mx[:].unsqueeze(2).to_broadcast([P, NT, E]),
+                                    op=ALU.subtract)
+            nc.scalar.activation(out=ex[:], in_=lg[:], func=ACT.Exp)
+
+        def softmax_second():
+            nc.vector.tensor_reduce(out=sm[:], in_=ex[:], axis=AX.X, op=ALU.add)
+            nc.vector.reciprocal(out=rs[:], in_=sm[:])
+            nc.vector.tensor_tensor(out=gate[:], in0=ex[:], in1=rs[:].unsqueeze(2).to_broadcast([P, NT, E]),
+                                    op=ALU.mult)
+
+        def gate_parts():
+            nc.vector.tensor_copy(out=gate_pad[:, :, 0:E], in_=gate[:])
+            nc.vector.tensor_tensor(out=gate_pad[:, :, E:2 * E], in0=gate[:], in1=gate_pad[:, :, 0:E],
+                                    op=ALU.subtract)
+            nc.vector.tensor_scalar_add(out=g3m1[:], in0=gate[:, :, 3], scalar1=-1.0)
+            nc.vector.tensor_copy(out=gate_pad[:, :, 8], in_=g3m1[:])
+            nc.vector.tensor_tensor(out=gate_pad[:, :, 9], in0=g3m1[:], in1=gate_pad[:, :, 8], op=ALU.subtract)
 
         for e in range(E):
             wg = stage.tile([P, M, 4], BF16, tag="wg", align_bytes=64)
@@ -149,117 +166,117 @@ def tile_dynamix_pb_t_kernel(tc, z, mlp_out, t2, A, W, h, out):
                                             ident_b[:])
                 dst = wg[:, 256 * half:256 * (half + 1), :].rearrange("p (a r) j -> p a r j", a=2)
                 src = xt[:].rearrange("p (a j) r -> p a r j", a=2)
-                if half == 0:
+                if half == 0 and e != 1:
                     nc.vector.tensor_copy(out=dst, in_=src)
                 else:
                     nc.scalar.copy(out=dst, in_=src)
             nc.vector.quantize_mx(out=wq[:, e, :].bitcast(FP8X4), scales=ws[:, e, :],
                                   in_=wg[:].rearrange("p m j -> p (m j)"))
-        relu_z(1)
-        relu_z(2)
-        regroup_z(1)
+            if e == 0:
+                softmax_first()
+            if e == 1:
+                softmax_second()
 
-        off_fields = {}
+        gate_banks = []
 
-        def off_tiles(g):
-            return [TPG * g + i for i in range(TPG - OFF_TILES[g], TPG)]
-
-        def gate_h_scalar(g):
-            for tb in off_tiles(g):
-                f0 = hfields.tile([P, M], F32, tag="h0")
-                f2 = hfields.tile([P, M], F32, tag="h2")
-                nc.scalar.activation(out=f0[:], in_=dh[:, 0, :], func=ACT.Copy, scale=gate[:, tb, 0:1])
-                nc.scalar.activation(out=f2[:], in_=dh[:, 2, :], func=ACT.Copy, scale=gate[:, tb, 2:3])
-                off_fields[tb] = [f0, f2]
-
-        def gate_h_vector(g):
-            for tb in off_tiles(g):
-                f0 = off_fields[tb][0]
-                nc.vector.scalar_tensor_tensor(out=f0[:], in0=dh[:, 1, :], scalar=gate[:, tb, 1:2], in1=f0[:],
-                                               op0=ALU.mult, op1=ALU.add)
-
-        group_fields = {}
-
-        def experts(g):
-            rows = []
-            for i in range(TPG):
-                tb = TPG * g + i
-                bs = slice(P * tb, P * (tb + 1))
-                acc = []
-                for e in range(E):
-                    pe = pp.tile([P, M], F32, tag="P")
-                    nc.tensor.matmul_mx(out=pe[:], lhsT=zq[:, bs].bitcast(FP8X4), lhsT_scale=zs[:, bs],
-                                        rhs=wq[:, e, :].bitcast(FP8X4), rhs_scale=ws[:, e, :],
-                                        start=True, stop=True)
-                    if e % 2 == 0:
-                        fld = fields.tile([P, M], F32, tag="f%d" % (e // 2))
-                        nc.scalar.activation(out=fld[:], in_=pe[:], func=ACT.Copy, scale=gate[:, tb, e:e + 1])
-                        acc.append(fld)
-                    else:
-                        fld = acc[-1]
-                        nc.vector.scalar_tensor_tensor(out=fld[:], in0=pe[:], scalar=gate[:, tb, e:e + 1],
-                                                       in1=fld[:], op0=ALU.mult, op1=ALU.add)
-                rows.append(acc)
-            group_fields[g] = rows
-
-        def finish(g):
-            gs = slice(GW * g, GW * (g + 1))
-            rows = group_fields[g]
-            wide = GW - P * OFF_TILES[g]
-            if g + 2 < NG:
-                regroup_z(g + 2)
-            if g + 1 < NG:
-                gate_h_scalar(g + 1)
-            todo = []
-            for i in range(TPG):
-                for fld in rows[i] + off_fields.get(TPG * g + i, []):
-                    todo.append((i, fld))
+        def gate_transposes():
+            for q in range(4):
+                wt = ps2.tile([P, 8, P], BF16, tag="b%d" % (1 + q % 2))
+                for i in range(8):
+                    nc.tensor.transpose(wt[:, i, :], gate_pad[:, 8 * q + i, :], ident_b[:])
+                gate_banks.append(wt)
+            ht = pp.tile([P, MT, P], BF16, tag="P")
             for mt in range(MT):
-                ms = slice(P * mt, P * (mt + 1))
-                b2 = ps2.tile([P, GW], F32, tag="b2")
-                nc.tensor.matmul(out=b2[:], lhsT=a_pad[:, ms], rhs=gate_rows[:, gs], start=True, stop=True)
-                b1 = ps2.tile([P, GW], F32, tag="b1")
-                nc.tensor.matmul(out=b1[:, 0:wide], lhsT=h_pad[:, ms],
-                                 rhs=gate_rows[:, GW * g:GW * g + wide], start=True, stop=False)
-                for n, (i, fld) in enumerate(todo):
-                    nc.tensor.matmul(out=b1[:, P * i:P * (i + 1)], lhsT=fld[:, ms], rhs=ident_f[:],
-                                     is_transpose=True, start=False, stop=(n == len(todo) - 1))
-                xs = outs.tile([P, GW], F32, tag="xs")
-                nc.vector.tensor_tensor(out=xs[:], in0=b2[:], in1=z_raw[:, 1 + mt, gs], op=ALU.mult)
-                nc.vector.scalar_tensor_tensor(out=xs[:], in0=b1[:], scalar=h_col[:, mt:mt + 1], in1=xs[:],
-                                               op0=ALU.add, op1=ALU.add)
-                nc.sync.dma_start(out=out[ms, gs], in_=xs[:])
-            if g + 1 < NG:
-                gate_h_vector(g + 1)
-            if g + 2 < NG:
-                quantise_z(g + 2)
-            if g + 3 < NG:
-                relu_z(g + 3)
+                nc.tensor.transpose(ht[:, mt, :], h_pad[:, P * mt:P * (mt + 1)], ident_b[:])
+            nc.vector.tensor_copy(out=h_col[:], in_=ht[:, :, 8])
 
-        experts(0)
+        def gate_copy(q):
+            nc.scalar.copy(out=gate_rows[:, 1024 * q:1024 * (q + 1)],
+                           in_=gate_banks[q][:].rearrange("p t c -> p (t c)"))
 
-        nc.vector.tensor_copy(out=gate_pad[:, :, 0:E], in_=gate[:])
-        nc.vector.tensor_tensor(out=gate_pad[:, :, E:2 * E], in0=gate[:], in1=gate_pad[:, :, 0:E],
-                                op=ALU.subtract)
-        nc.vector.tensor_scalar_add(out=g3m1[:], in0=gate[:, :, 3], scalar1=-1.0)
-        nc.vector.tensor_copy(out=gate_pad[:, :, 8], in_=g3m1[:])
-        nc.vector.tensor_tensor(out=gate_pad[:, :, 9], in0=g3m1[:], in1=gate_pad[:, :, 8], op=ALU.subtract)
-        for q in range(4):
-            wt = ps2.tile([P, 8, P], BF16, tag="b1")
-            for i in range(8):
-                nc.tensor.transpose(wt[:, i, :], gate_pad[:, 8 * q + i, :], ident_b[:])
-            nc.scalar.copy(out=gate_rows[:, 1024 * q:1024 * (q + 1)], in_=wt[:].rearrange("p t c -> p (t c)"))
-        ht = ps2.tile([P, MT, P], BF16, tag="b2")
-        for mt in range(MT):
-            nc.tensor.transpose(ht[:, mt, :], h_pad[:, P * mt:P * (mt + 1)], ident_b[:])
-        nc.vector.tensor_copy(out=h_col[:], in_=ht[:, :, 8])
-        quantise_z(1)
-        nc.vector.tensor_tensor(out=dh[:], in0=h_bc[:, 0:3, :], in1=h_bc[:, 3:4, :].to_broadcast([P, E - 1, M]),
-                                op=ALU.subtract)
-        gate_h_scalar(0)
-        gate_h_vector(0)
+        relu_z(0)
+        for tb in range(AHEAD_COPY):
+            regroup_z(tb)
+            if tb < AHEAD_QUANT:
+                quantise_z(tb)
 
+        for e in range(E - 1):
+            nc.gpsimd.tensor_tensor(out=dh[:, e, :], in0=h_bc[:, e, :], in1=h_bc[:, 3, :], op=ALU.subtract)
+        pool_h = {}
         for g in range(NG):
-            if g + 1 < NG:
-                experts(g + 1)
-            finish(g)
+            for i in range(TPG - OFF_TILES[g], TPG):
+                tb = TPG * g + i
+                gh = keep.tile([P, M], F32, name="gh%d" % tb)
+                nc.gpsimd.tensor_scalar(out=gh[:], in0=dh[:, 0, :], scalar1=gate[:, tb, 0:1], scalar2=0.0,
+                                        op0=ALU.mult, op1=ALU.add)
+                for e in range(1, E - 1):
+                    tm = stage.tile([P, M], F32, tag="tm")
+                    nc.gpsimd.tensor_scalar(out=tm[:], in0=dh[:, e, :], scalar1=gate[:, tb, e:e + 1], scalar2=0.0,
+                                            op0=ALU.mult, op1=ALU.add)
+                    nc.gpsimd.tensor_tensor(out=gh[:], in0=gh[:], in1=tm[:], op=ALU.add)
+                pool_h[tb] = gh
+
+        tile_fields = {}
+
+        def experts(tb):
+            bs = slice(P * tb, P * (tb + 1))
+            on_scalar = scalar_experts(tb)
+            on_vector = [e for e in range(E) if e not in on_scalar]
+            banks = {}
+            for e in on_scalar + on_vector:
+                pe = pp.tile([P, M], F32, tag="P")
+                nc.tensor.matmul_mx(out=pe[:], lhsT=zq[:, bs].bitcast(FP8X4), lhsT_scale=zs[:, bs],
+                                    rhs=wq[:, e, :].bitcast(FP8X4), rhs_scale=ws[:, e, :],
+                                    start=True, stop=True)
+                banks[e] = pe
+            acc = []
+            for n, e in enumerate(on_scalar):
+                fld = fields.tile([P, M], F32, tag="f%d" % n)
+                nc.scalar.activation(out=fld[:], in_=banks[e][:], func=ACT.Copy, scale=gate[:, tb, e:e + 1])
+                acc.append(fld)
+            for n, e in enumerate(on_vector):
+                fld = acc[n % len(acc)]
+                nc.vector.scalar_tensor_tensor(out=fld[:], in0=banks[e][:], scalar=gate[:, tb, e:e + 1],
+                                               in1=fld[:], op0=ALU.mult, op1=ALU.add)
+            if tb in pool_h:
+                acc.append(pool_h[tb])
+            tile_fields[tb] = acc
+
+        def finish(g, mt):
+            gs = slice(GW * g, GW * (g + 1))
+            ms = slice(P * mt, P * (mt + 1))
+            wide = GW - P * OFF_TILES[g]
+            todo = [(i, fld) for i in range(TPG) for fld in tile_fields[TPG * g + i]]
+            b2 = ps2.tile([P, GW], F32, tag="b2")
+            nc.tensor.matmul(out=b2[:], lhsT=a_pad[:, ms], rhs=gate_rows[:, gs], start=True, stop=True)
+            b1 = ps2.tile([P, GW], F32, tag="b1")
+            nc.tensor.matmul(out=b1[:, 0:wide], lhsT=h_pad[:, ms],
+                             rhs=gate_rows[:, GW * g:GW * g + wide], start=True, stop=False)
+            for n, (i, fld) in enumerate(todo):
+                nc.tensor.matmul(out=b1[:, P * i:P * (i + 1)], lhsT=fld[:, ms], rhs=ident_f[:],
+                                 is_transpose=True, start=False, stop=(n == len(todo) - 1))
+            xs = outs.tile([P, GW], F32, tag="xs")
+            nc.vector.tensor_tensor(out=xs[:], in0=b2[:], in1=z_raw[:, 1 + mt, gs], op=ALU.mult)
+            nc.vector.scalar_tensor_tensor(out=xs[:], in0=b1[:], scalar=h_col[:, mt:mt + 1], in1=xs[:],
+                                           op0=ALU.add, op1=ALU.add)
+            nc.sync.dma_start(out=out[ms, gs], in_=xs[:])
+
+        for s in range(NT + LAG):
+            if s < NT:
+                experts(s)
+            if s == 0:
+                gate_parts()
+            if s == 1:
+                gate_transposes()
+            if s in (2, 3):
+                gate_copy(2 * s - 4)
+                gate_copy(2 * s - 3)
+            nxt = s + AHEAD_COPY
+            if nxt < NT:
+                if nxt % TPG == 0:
+                    relu_z(nxt // TPG)
+                regroup_z(nxt)
+            if s >= LAG:
+                finish((s - LAG) // MT, (s - LAG) % MT)
+            if s + AHEAD_QUANT < NT:
+                quantise_z(s + AHEAD_QUANT)

@@ -27,6 +27,7 @@ LAG = 4
 AHEAD_COPY = 3
 AHEAD_QUANT = 2
 FIELD_BUFS = 10
+FIRST_PRODUCT = 3
 
 FLOPS = 2 * E * M * M * B
 
@@ -43,6 +44,7 @@ def tile_dynamix_pb_t_kernel(tc, z, mlp_out, t2, A, W, h, out):
         stage = ctx.enter_context(tc.tile_pool(name="stage", bufs=2))
         zstage = ctx.enter_context(tc.tile_pool(name="zstage", bufs=6))
         fields = ctx.enter_context(tc.tile_pool(name="fields", bufs=FIELD_BUFS))
+        hfields = ctx.enter_context(tc.tile_pool(name="hfields", bufs=12))
         outs = ctx.enter_context(tc.tile_pool(name="outs", bufs=6))
         pp = ctx.enter_context(tc.psum_pool(name="pp", bufs=4))
         ps2 = ctx.enter_context(tc.psum_pool(name="ps2", bufs=2))
@@ -92,10 +94,9 @@ def tile_dynamix_pb_t_kernel(tc, z, mlp_out, t2, A, W, h, out):
             )
         load_z(0)
         load_z(1)
-        load_z(2)
         nc.sync.dma_start(out=h_bc[:].rearrange("p e m -> p (e m)"),
                           in_=h.rearrange("e m -> (e m)").partition_broadcast(P))
-        for g in range(3, NG):
+        for g in range(2, NG):
             load_z(g)
 
         nc.vector.memset(warm[:], 0.0)
@@ -202,19 +203,14 @@ def tile_dynamix_pb_t_kernel(tc, z, mlp_out, t2, A, W, h, out):
 
         for e in range(E - 1):
             nc.gpsimd.tensor_tensor(out=dh[:, e, :], in0=h_bc[:, e, :], in1=h_bc[:, 3, :], op=ALU.subtract)
-        pool_h = {}
-        for g in range(NG):
-            for i in range(TPG - OFF_TILES[g], TPG):
-                tb = TPG * g + i
-                gh = keep.tile([P, M], F32, name="gh%d" % tb)
-                nc.gpsimd.tensor_scalar(out=gh[:], in0=dh[:, 0, :], scalar1=gate[:, tb, 0:1], scalar2=0.0,
-                                        op0=ALU.mult, op1=ALU.add)
-                for e in range(1, E - 1):
-                    tm = stage.tile([P, M], F32, tag="tm")
-                    nc.gpsimd.tensor_scalar(out=tm[:], in0=dh[:, e, :], scalar1=gate[:, tb, e:e + 1], scalar2=0.0,
-                                            op0=ALU.mult, op1=ALU.add)
-                    nc.gpsimd.tensor_tensor(out=gh[:], in0=gh[:], in1=tm[:], op=ALU.add)
-                pool_h[tb] = gh
+        off_tiles = [TPG * g + i for g in range(NG) for i in range(TPG - OFF_TILES[g], TPG)]
+        products = [(tb, e) for tb in off_tiles for e in (0, 2)]
+        product_fields = {}
+
+        def make_product(tb, e):
+            fld = hfields.tile([P, M], F32, tag="hd")
+            nc.scalar.activation(out=fld[:], in_=dh[:, e, :], func=ACT.Copy, scale=gate[:, tb, e:e + 1])
+            product_fields[tb] = product_fields.get(tb, []) + [fld]
 
         tile_fields = {}
 
@@ -238,15 +234,17 @@ def tile_dynamix_pb_t_kernel(tc, z, mlp_out, t2, A, W, h, out):
                 fld = acc[n % len(acc)]
                 nc.vector.scalar_tensor_tensor(out=fld[:], in0=banks[e][:], scalar=gate[:, tb, e:e + 1],
                                                in1=fld[:], op0=ALU.mult, op1=ALU.add)
-            if tb in pool_h:
-                acc.append(pool_h[tb])
+            if tb in off_tiles:
+                nc.vector.scalar_tensor_tensor(out=acc[0][:], in0=dh[:, 1, :], scalar=gate[:, tb, 1:2],
+                                               in1=acc[0][:], op0=ALU.mult, op1=ALU.add)
             tile_fields[tb] = acc
 
         def finish(g, mt):
             gs = slice(GW * g, GW * (g + 1))
             ms = slice(P * mt, P * (mt + 1))
             wide = GW - P * OFF_TILES[g]
-            todo = [(i, fld) for i in range(TPG) for fld in tile_fields[TPG * g + i]]
+            todo = [(i, fld) for i in range(TPG)
+                    for fld in tile_fields[TPG * g + i] + product_fields.get(TPG * g + i, [])]
             b2 = ps2.tile([P, GW], F32, tag="b2")
             nc.tensor.matmul(out=b2[:], lhsT=a_pad[:, ms], rhs=gate_rows[:, gs], start=True, stop=True)
             b1 = ps2.tile([P, GW], F32, tag="b1")
@@ -276,6 +274,8 @@ def tile_dynamix_pb_t_kernel(tc, z, mlp_out, t2, A, W, h, out):
                 if nxt % TPG == 0:
                     relu_z(nxt // TPG)
                 regroup_z(nxt)
+            if 0 <= s - FIRST_PRODUCT < len(products):
+                make_product(products[s - FIRST_PRODUCT][0], products[s - FIRST_PRODUCT][1])
             if s >= LAG:
                 finish((s - LAG) // MT, (s - LAG) % MT)
             if s + AHEAD_QUANT < NT:

@@ -24,16 +24,12 @@ TPG = GW // P
 MT = M // P
 OFF_TILES = [0, 1, 2, 2, 2, 2, 2, 2]
 LAG = 4
-AHEAD_COPY = 3
-AHEAD_QUANT = 2
+AHEAD = 3
 FIELD_BUFS = 10
 FIRST_PRODUCT = 3
+BANKS = 8
 
 FLOPS = 2 * E * M * M * B
-
-
-def scalar_experts(tb):
-    return [0] if tb < TPG else [0, 2]
 
 
 def tile_dynamix_pb_t_kernel(tc, z, mlp_out, t2, A, W, h, out):
@@ -46,8 +42,13 @@ def tile_dynamix_pb_t_kernel(tc, z, mlp_out, t2, A, W, h, out):
         fields = ctx.enter_context(tc.tile_pool(name="fields", bufs=FIELD_BUFS))
         hfields = ctx.enter_context(tc.tile_pool(name="hfields", bufs=12))
         outs = ctx.enter_context(tc.tile_pool(name="outs", bufs=6))
-        pp = ctx.enter_context(tc.psum_pool(name="pp", bufs=4))
-        ps2 = ctx.enter_context(tc.psum_pool(name="ps2", bufs=2))
+        psum = ctx.enter_context(tc.psum_pool(name="psum", bufs=1))
+        bank_uses = []
+
+        def bank(shape, dtype):
+            n = len(bank_uses)
+            bank_uses.append(n)
+            return psum.tile(shape, dtype, tag="bank%d" % (n % BANKS), name="use%d" % n)
 
         z_raw = keep.tile([P, 5, B], BF16, name="z_raw")
         zq = keep.tile([P, B], U32, name="zq", align_bytes=64)
@@ -158,7 +159,7 @@ def tile_dynamix_pb_t_kernel(tc, z, mlp_out, t2, A, W, h, out):
         for e in range(E):
             wg = stage.tile([P, M, 4], BF16, tag="wg", align_bytes=64)
             for half in range(2):
-                xt = pp.tile([P, 8, P], BF16, tag="P")
+                xt = bank([P, 8, P], BF16)
                 for a in range(2):
                     mt = 2 * half + a
                     for j in range(4):
@@ -178,28 +179,23 @@ def tile_dynamix_pb_t_kernel(tc, z, mlp_out, t2, A, W, h, out):
             if e == 1:
                 softmax_second()
 
-        gate_banks = []
+        def gate_quarter(q):
+            wt = bank([P, 8, P], BF16)
+            for i in range(8):
+                nc.tensor.transpose(wt[:, i, :], gate_pad[:, 8 * q + i, :], ident_b[:])
+            nc.vector.tensor_copy(out=gate_rows[:, 1024 * q:1024 * (q + 1)],
+                                  in_=wt[:].rearrange("p t c -> p (t c)"))
 
-        def gate_transposes():
-            for q in range(4):
-                wt = ps2.tile([P, 8, P], BF16, tag="b%d" % (1 + q % 2))
-                for i in range(8):
-                    nc.tensor.transpose(wt[:, i, :], gate_pad[:, 8 * q + i, :], ident_b[:])
-                gate_banks.append(wt)
-            ht = pp.tile([P, MT, P], BF16, tag="P")
+        def h3_column():
+            ht = bank([P, MT, P], BF16)
             for mt in range(MT):
                 nc.tensor.transpose(ht[:, mt, :], h_pad[:, P * mt:P * (mt + 1)], ident_b[:])
             nc.vector.tensor_copy(out=h_col[:], in_=ht[:, :, 8])
 
-        def gate_copy(q):
-            nc.scalar.copy(out=gate_rows[:, 1024 * q:1024 * (q + 1)],
-                           in_=gate_banks[q][:].rearrange("p t c -> p (t c)"))
-
         relu_z(0)
-        for tb in range(AHEAD_COPY):
+        for tb in range(AHEAD - 1):
             regroup_z(tb)
-            if tb < AHEAD_QUANT:
-                quantise_z(tb)
+            quantise_z(tb)
 
         for e in range(E - 1):
             nc.gpsimd.tensor_tensor(out=dh[:, e, :], in0=h_bc[:, e, :], in1=h_bc[:, 3, :], op=ALU.subtract)
@@ -212,71 +208,100 @@ def tile_dynamix_pb_t_kernel(tc, z, mlp_out, t2, A, W, h, out):
             nc.scalar.activation(out=fld[:], in_=dh[:, e, :], func=ACT.Copy, scale=gate[:, tb, e:e + 1])
             product_fields[tb] = product_fields.get(tb, []) + [fld]
 
+        banks = {}
         tile_fields = {}
+        unit_banks = {}
+        unit_out = {}
 
-        def experts(tb):
+        def mx_pass(tb, e):
             bs = slice(P * tb, P * (tb + 1))
-            on_scalar = scalar_experts(tb)
-            on_vector = [e for e in range(E) if e not in on_scalar]
-            banks = {}
-            for e in on_scalar + on_vector:
-                pe = pp.tile([P, M], F32, tag="P")
-                nc.tensor.matmul_mx(out=pe[:], lhsT=zq[:, bs].bitcast(FP8X4), lhsT_scale=zs[:, bs],
-                                    rhs=wq[:, e, :].bitcast(FP8X4), rhs_scale=ws[:, e, :],
-                                    start=True, stop=True)
-                banks[e] = pe
-            acc = []
-            for n, e in enumerate(on_scalar):
-                fld = fields.tile([P, M], F32, tag="f%d" % n)
-                nc.scalar.activation(out=fld[:], in_=banks[e][:], func=ACT.Copy, scale=gate[:, tb, e:e + 1])
-                acc.append(fld)
-            for n, e in enumerate(on_vector):
-                fld = acc[n % len(acc)]
-                nc.vector.scalar_tensor_tensor(out=fld[:], in0=banks[e][:], scalar=gate[:, tb, e:e + 1],
-                                               in1=fld[:], op0=ALU.mult, op1=ALU.add)
-            if tb in off_tiles:
-                nc.vector.scalar_tensor_tensor(out=acc[0][:], in0=dh[:, 1, :], scalar=gate[:, tb, 1:2],
-                                               in1=acc[0][:], op0=ALU.mult, op1=ALU.add)
-            tile_fields[tb] = acc
+            pe = bank([P, M], F32)
+            nc.tensor.matmul_mx(out=pe[:], lhsT=zq[:, bs].bitcast(FP8X4), lhsT_scale=zs[:, bs],
+                                rhs=wq[:, e, :].bitcast(FP8X4), rhs_scale=ws[:, e, :],
+                                start=True, stop=True)
+            banks[(tb, e)] = pe
 
-        def finish(g, mt):
+        def scalar_exit(tb, e):
+            fld = fields.tile([P, M], F32, tag="f%d" % (e // 2))
+            nc.scalar.activation(out=fld[:], in_=banks[(tb, e)][:], func=ACT.Copy, scale=gate[:, tb, e:e + 1])
+            tile_fields[tb] = tile_fields.get(tb, []) + [fld]
+
+        def vector_exit(tb, e):
+            fld = tile_fields[tb][e // 2]
+            nc.vector.scalar_tensor_tensor(out=fld[:], in0=banks[(tb, e)][:], scalar=gate[:, tb, e:e + 1],
+                                           in1=fld[:], op0=ALU.mult, op1=ALU.add)
+
+        def vector_product(tb):
+            fld = tile_fields[tb][0]
+            nc.vector.scalar_tensor_tensor(out=fld[:], in0=dh[:, 1, :], scalar=gate[:, tb, 1:2],
+                                           in1=fld[:], op0=ALU.mult, op1=ALU.add)
+
+        def plain_part(u):
+            g, mt = u // MT, u % MT
             gs = slice(GW * g, GW * (g + 1))
             ms = slice(P * mt, P * (mt + 1))
             wide = GW - P * OFF_TILES[g]
             todo = [(i, fld) for i in range(TPG)
                     for fld in tile_fields[TPG * g + i] + product_fields.get(TPG * g + i, [])]
-            b2 = ps2.tile([P, GW], F32, tag="b2")
+            b2 = bank([P, GW], F32)
             nc.tensor.matmul(out=b2[:], lhsT=a_pad[:, ms], rhs=gate_rows[:, gs], start=True, stop=True)
-            b1 = ps2.tile([P, GW], F32, tag="b1")
+            b1 = bank([P, GW], F32)
             nc.tensor.matmul(out=b1[:, 0:wide], lhsT=h_pad[:, ms],
                              rhs=gate_rows[:, GW * g:GW * g + wide], start=True, stop=False)
             for n, (i, fld) in enumerate(todo):
                 nc.tensor.matmul(out=b1[:, P * i:P * (i + 1)], lhsT=fld[:, ms], rhs=ident_f[:],
                                  is_transpose=True, start=False, stop=(n == len(todo) - 1))
-            xs = outs.tile([P, GW], F32, tag="xs")
-            nc.vector.tensor_tensor(out=xs[:], in0=b2[:], in1=z_raw[:, 1 + mt, gs], op=ALU.mult)
-            nc.vector.scalar_tensor_tensor(out=xs[:], in0=b1[:], scalar=h_col[:, mt:mt + 1], in1=xs[:],
-                                           op0=ALU.add, op1=ALU.add)
-            nc.sync.dma_start(out=out[ms, gs], in_=xs[:])
+            unit_banks[u] = (b2, b1)
 
-        for s in range(NT + LAG):
-            if s < NT:
-                experts(s)
-            if s == 0:
-                gate_parts()
-            if s == 1:
-                gate_transposes()
-            if s in (2, 3):
-                gate_copy(2 * s - 4)
-                gate_copy(2 * s - 3)
-            nxt = s + AHEAD_COPY
+        def times_z(u):
+            g, mt = u // MT, u % MT
+            xs = outs.tile([P, GW], F32, tag="xs")
+            nc.vector.tensor_tensor(out=xs[:], in0=unit_banks[u][0][:],
+                                    in1=z_raw[:, 1 + mt, GW * g:GW * (g + 1)], op=ALU.mult)
+            unit_out[u] = xs
+
+        def last_add(u):
+            g, mt = u // MT, u % MT
+            xs = unit_out[u]
+            nc.vector.scalar_tensor_tensor(out=xs[:], in0=unit_banks[u][1][:], scalar=h_col[:, mt:mt + 1],
+                                           in1=xs[:], op0=ALU.add, op1=ALU.add)
+            nc.sync.dma_start(out=out[P * mt:P * (mt + 1), GW * g:GW * (g + 1)], in_=xs[:])
+
+        UNITS = NG * MT
+        for s in range(-1, NT + LAG + 1):
+            u = s - LAG
+            for e_scalar, e_vector in ((0, 1), (2, 3)):
+                if s + 1 < NT:
+                    mx_pass(s + 1, e_scalar)
+                if 0 <= s < NT:
+                    mx_pass(s, e_vector)
+            if 0 <= u < UNITS:
+                plain_part(u)
+            if s + 1 < NT:
+                scalar_exit(s + 1, 0)
+                scalar_exit(s + 1, 2)
+            nxt = s + AHEAD
             if nxt < NT:
                 if nxt % TPG == 0:
                     relu_z(nxt // TPG)
                 regroup_z(nxt)
             if 0 <= s - FIRST_PRODUCT < len(products):
                 make_product(products[s - FIRST_PRODUCT][0], products[s - FIRST_PRODUCT][1])
-            if s >= LAG:
-                finish((s - LAG) // MT, (s - LAG) % MT)
-            if s + AHEAD_QUANT < NT:
-                quantise_z(s + AHEAD_QUANT)
+            if 0 <= u - 1 < UNITS:
+                last_add(u - 1)
+            if 0 <= s < NT:
+                vector_exit(s, 1)
+                vector_exit(s, 3)
+                if s in off_tiles:
+                    vector_product(s)
+            if 0 <= u < UNITS:
+                times_z(u)
+            if s == -1:
+                gate_parts()
+            if s == 0:
+                gate_quarter(0)
+                h3_column()
+            if 1 <= s <= 3:
+                gate_quarter(s)
+            if nxt < NT:
+                quantise_z(nxt)

@@ -24,9 +24,9 @@ TPG = GW // P
 MT = M // P
 OFF_TILES = [0, 1, 2, 2, 2, 2, 2, 2]
 LAG = 4
-AHEAD = 3
+AHEAD_COPY = 4
+AHEAD_QUANT = 3
 FIELD_BUFS = 10
-FIRST_PRODUCT = 3
 BANKS = 8
 
 FLOPS = 2 * E * M * M * B
@@ -40,7 +40,6 @@ def tile_dynamix_pb_t_kernel(tc, z, mlp_out, t2, A, W, h, out):
         stage = ctx.enter_context(tc.tile_pool(name="stage", bufs=2))
         zstage = ctx.enter_context(tc.tile_pool(name="zstage", bufs=6))
         fields = ctx.enter_context(tc.tile_pool(name="fields", bufs=FIELD_BUFS))
-        hfields = ctx.enter_context(tc.tile_pool(name="hfields", bufs=12))
         outs = ctx.enter_context(tc.tile_pool(name="outs", bufs=6))
         psum = ctx.enter_context(tc.psum_pool(name="psum", bufs=1))
         bank_uses = []
@@ -193,20 +192,25 @@ def tile_dynamix_pb_t_kernel(tc, z, mlp_out, t2, A, W, h, out):
             nc.vector.tensor_copy(out=h_col[:], in_=ht[:, :, 8])
 
         relu_z(0)
-        for tb in range(AHEAD - 1):
+        for tb in range(AHEAD_COPY - 1):
             regroup_z(tb)
-            quantise_z(tb)
+            if tb < AHEAD_QUANT - 1:
+                quantise_z(tb)
 
         for e in range(E - 1):
             nc.gpsimd.tensor_tensor(out=dh[:, e, :], in0=h_bc[:, e, :], in1=h_bc[:, 3, :], op=ALU.subtract)
         off_tiles = [TPG * g + i for g in range(NG) for i in range(TPG - OFF_TILES[g], TPG)]
-        products = [(tb, e) for tb in off_tiles for e in (0, 2)]
         product_fields = {}
-
-        def make_product(tb, e):
-            fld = hfields.tile([P, M], F32, tag="hd")
-            nc.scalar.activation(out=fld[:], in_=dh[:, e, :], func=ACT.Copy, scale=gate[:, tb, e:e + 1])
-            product_fields[tb] = product_fields.get(tb, []) + [fld]
+        for tb in off_tiles:
+            gh = keep.tile([P, M], F32, name="gh%d" % tb)
+            nc.gpsimd.tensor_scalar(out=gh[:], in0=dh[:, 0, :], scalar1=gate[:, tb, 0:1], scalar2=0.0,
+                                    op0=ALU.mult, op1=ALU.add)
+            for e in range(1, E - 1):
+                tm = stage.tile([P, M], F32, tag="tm")
+                nc.gpsimd.tensor_scalar(out=tm[:], in0=dh[:, e, :], scalar1=gate[:, tb, e:e + 1], scalar2=0.0,
+                                        op0=ALU.mult, op1=ALU.add)
+                nc.gpsimd.tensor_tensor(out=gh[:], in0=gh[:], in1=tm[:], op=ALU.add)
+            product_fields[tb] = [gh]
 
         banks = {}
         tile_fields = {}
@@ -229,11 +233,6 @@ def tile_dynamix_pb_t_kernel(tc, z, mlp_out, t2, A, W, h, out):
         def vector_exit(tb, e):
             fld = tile_fields[tb][e // 2]
             nc.vector.scalar_tensor_tensor(out=fld[:], in0=banks[(tb, e)][:], scalar=gate[:, tb, e:e + 1],
-                                           in1=fld[:], op0=ALU.mult, op1=ALU.add)
-
-        def vector_product(tb):
-            fld = tile_fields[tb][0]
-            nc.vector.scalar_tensor_tensor(out=fld[:], in0=dh[:, 1, :], scalar=gate[:, tb, 1:2],
                                            in1=fld[:], op0=ALU.mult, op1=ALU.add)
 
         def plain_part(u):
@@ -280,20 +279,16 @@ def tile_dynamix_pb_t_kernel(tc, z, mlp_out, t2, A, W, h, out):
             if s + 1 < NT:
                 scalar_exit(s + 1, 0)
                 scalar_exit(s + 1, 2)
-            nxt = s + AHEAD
+            nxt = s + AHEAD_COPY
             if nxt < NT:
                 if nxt % TPG == 0:
                     relu_z(nxt // TPG)
                 regroup_z(nxt)
-            if 0 <= s - FIRST_PRODUCT < len(products):
-                make_product(products[s - FIRST_PRODUCT][0], products[s - FIRST_PRODUCT][1])
             if 0 <= u - 1 < UNITS:
                 last_add(u - 1)
             if 0 <= s < NT:
                 vector_exit(s, 1)
                 vector_exit(s, 3)
-                if s in off_tiles:
-                    vector_product(s)
             if 0 <= u < UNITS:
                 times_z(u)
             if s == -1:
@@ -303,5 +298,5 @@ def tile_dynamix_pb_t_kernel(tc, z, mlp_out, t2, A, W, h, out):
                 h3_column()
             if 1 <= s <= 3:
                 gate_quarter(s)
-            if nxt < NT:
-                quantise_z(nxt)
+            if s + AHEAD_QUANT < NT:
+                quantise_z(s + AHEAD_QUANT)

@@ -155,8 +155,10 @@ def tile_dynamix_pb_t_kernel(tc, z, mlp_out, t2, A, W, h, out):
             nc.vector.tensor_copy(out=gate_pad[:, :, 8], in_=g3m1[:])
             nc.vector.tensor_tensor(out=gate_pad[:, :, 9], in0=g3m1[:], in1=gate_pad[:, :, 8], op=ALU.subtract)
 
+        w_banks = {}
+        w_grouped = {}
         for e in range(E):
-            wg = stage.tile([P, M, 4], BF16, tag="wg", align_bytes=64)
+            w_grouped[e] = keep.tile([P, M, 4], BF16, name="wg%d" % e, align_bytes=64)
             for half in range(2):
                 xt = bank([P, 8, P], BF16)
                 for a in range(2):
@@ -165,18 +167,40 @@ def tile_dynamix_pb_t_kernel(tc, z, mlp_out, t2, A, W, h, out):
                         t = (j + 3) % 4
                         nc.tensor.transpose(xt[:, 4 * a + j, :], w_raw[:, MT * e + mt, P * t:P * (t + 1)],
                                             ident_b[:])
-                dst = wg[:, 256 * half:256 * (half + 1), :].rearrange("p (a r) j -> p a r j", a=2)
-                src = xt[:].rearrange("p (a j) r -> p a r j", a=2)
-                if half == 0 and e != 1:
-                    nc.vector.tensor_copy(out=dst, in_=src)
-                else:
-                    nc.scalar.copy(out=dst, in_=src)
+                w_banks[(e, half)] = xt
+
+        def w_exit(e, half, on_vector):
+            dst = w_grouped[e][:, 256 * half:256 * (half + 1), :].rearrange("p (a r) j -> p a r j", a=2)
+            src = w_banks[(e, half)][:].rearrange("p (a j) r -> p a r j", a=2)
+            if on_vector:
+                nc.vector.tensor_copy(out=dst, in_=src)
+            else:
+                nc.scalar.copy(out=dst, in_=src)
+
+        def w_quantise(e):
             nc.vector.quantize_mx(out=wq[:, e, :].bitcast(FP8X4), scales=ws[:, e, :],
-                                  in_=wg[:].rearrange("p m j -> p (m j)"))
-            if e == 0:
-                softmax_first()
-            if e == 1:
-                softmax_second()
+                                  in_=w_grouped[e][:].rearrange("p m j -> p (m j)"))
+
+        w_exit(0, 1, True)
+        w_exit(0, 0, False)
+        w_exit(1, 0, True)
+        w_exit(1, 1, False)
+        w_quantise(0)
+        w_exit(2, 1, False)
+        softmax_first()
+        w_exit(2, 0, True)
+        relu_z(0)
+        w_quantise(1)
+        regroup_z(0)
+        w_quantise(2)
+        regroup_z(1)
+        softmax_second()
+        w_exit(3, 0, False)
+        quantise_z(0)
+        regroup_z(2)
+        w_exit(3, 1, True)
+        quantise_z(1)
+        w_quantise(3)
 
         def gate_quarter(q):
             wt = bank([P, 8, P], BF16)
@@ -190,12 +214,6 @@ def tile_dynamix_pb_t_kernel(tc, z, mlp_out, t2, A, W, h, out):
             for mt in range(MT):
                 nc.tensor.transpose(ht[:, mt, :], h_pad[:, P * mt:P * (mt + 1)], ident_b[:])
             nc.vector.tensor_copy(out=h_col[:], in_=ht[:, :, 8])
-
-        relu_z(0)
-        for tb in range(AHEAD_COPY - 1):
-            regroup_z(tb)
-            if tb < AHEAD_QUANT - 1:
-                quantise_z(tb)
 
         for e in range(E - 1):
             nc.gpsimd.tensor_tensor(out=dh[:, e, :], in0=h_bc[:, e, :], in1=h_bc[:, 3, :], op=ALU.subtract)

@@ -65,7 +65,7 @@ def tile_dynamix_pb_t_kernel(tc, z, mlp_out, t2, A, W, h, out):
         ident_f = keep.tile([P, P], F32, name="ident_f")
         ident_b = keep.tile([P, P], BF16, name="ident_b")
         warm = keep.tile([P, 1], F32, name="warm")
-        ml = keep.tile([P, NT, E], BF16, name="ml")
+        ml_rows = keep.tile([P, P * E], BF16, name="ml_rows")
         t2b = keep.tile([P, 1], BF16, name="t2b")
         t2f = keep.tile([P, 1], F32, name="t2f")
         rinv = keep.tile([P, 1], F32, name="rinv")
@@ -84,9 +84,9 @@ def tile_dynamix_pb_t_kernel(tc, z, mlp_out, t2, A, W, h, out):
             nc.sync.dma_start(out=z_raw[:, 0, gs], in_=z_view[:, 3, gs])
             nc.sync.dma_start(out=z_raw[:, 1:5, gs], in_=z_view[:, :, gs])
 
-        with nc.allow_non_contiguous_dma(reason="gate logits: 8-byte rows"):
+        nc.scalar.dma_start(out=ml_rows[0:NT, :], in_=mlp_out.rearrange("(t p) e -> t (p e)", p=P))
+        with nc.allow_non_contiguous_dma(reason="one value to every partition"):
             nc.scalar.dma_start(out=t2b[:], in_=t2.partition_broadcast(P))
-            nc.scalar.dma_start(out=ml[:], in_=mlp_out.rearrange("(t p) e -> p t e", p=P))
         for e in range(E):
             nc.sync.dma_start(
                 out=w_raw[:, MT * e:MT * (e + 1), :],
@@ -99,6 +99,8 @@ def tile_dynamix_pb_t_kernel(tc, z, mlp_out, t2, A, W, h, out):
         for g in range(2, NG):
             load_z(g)
 
+        nc.vector.memset(ml_rows[32:64, :].bitcast(I32), 0)
+        nc.vector.memset(ml_rows[64:128, :].bitcast(I32), 0)
         nc.vector.memset(warm[:], 0.0)
         nc.scalar.activation(out=warm[:], in_=warm[:], func=ACT.Exp)
         nc.vector.memset(a_pad[:].bitcast(I32), 0)
@@ -134,8 +136,8 @@ def tile_dynamix_pb_t_kernel(tc, z, mlp_out, t2, A, W, h, out):
         def softmax_first():
             nc.vector.tensor_copy(out=t2f[:], in_=t2b[:])
             nc.vector.reciprocal(out=rinv[:], in_=t2f[:])
-            nc.vector.tensor_scalar(out=lg[:], in0=ml[:], scalar1=rinv[:, 0:1], scalar2=-1.0,
-                                    op0=ALU.mult, op1=ALU.mult)
+            nc.vector.tensor_scalar(out=lg[:], in0=ml_cols[:, :, 0:NT].rearrange("p e t -> p t e"),
+                                    scalar1=rinv[:, 0:1], scalar2=-1.0, op0=ALU.mult, op1=ALU.mult)
             nc.vector.tensor_reduce(out=mx[:], in_=lg[:], axis=AX.X, op=ALU.max)
             nc.vector.tensor_tensor(out=lg[:], in0=lg[:], in1=mx[:].unsqueeze(2).to_broadcast([P, NT, E]),
                                     op=ALU.subtract)
@@ -154,6 +156,10 @@ def tile_dynamix_pb_t_kernel(tc, z, mlp_out, t2, A, W, h, out):
             nc.vector.tensor_scalar_add(out=g3m1[:], in0=gate[:, :, 3], scalar1=-1.0)
             nc.vector.tensor_copy(out=gate_pad[:, :, 8], in_=g3m1[:])
             nc.vector.tensor_tensor(out=gate_pad[:, :, 9], in0=g3m1[:], in1=gate_pad[:, :, 8], op=ALU.subtract)
+
+        ml_cols = bank([P, E, P], BF16)
+        for e in range(E):
+            nc.tensor.transpose(ml_cols[:, e, :], ml_rows[:].rearrange("t (p e) -> t e p", e=E)[:, e, :], ident_b[:])
 
         w_banks = {}
         w_grouped = {}

from contextlib import ExitStack

import concourse.mybir as mybir
from concourse.masks import make_identity

F32 = mybir.dt.float32
BF16 = mybir.dt.bfloat16
I32 = mybir.dt.int32
U32 = mybir.dt.uint32
U8 = mybir.dt.uint8
FP8X4 = mybir.dt.float8_e4m3fn_x4
ALU = mybir.AluOpType
ACT = mybir.ActivationFunctionType
AX = mybir.AxisListType

P = 128
M = 512
B = 4096
E = 4
NT = B // P
GW = 512
NG = B // GW
TPG = GW // P
MT = M // P
OFF_TILES = [0, 1, 2, 2, 2, 2, 2, 2]
LAG = 4
AHEAD_COPY = 4
AHEAD_QUANT = 3
FIELD_BUFS = 10
BANKS = 8

FLOPS = 2 * E * M * M * B


def tile_dynamix_pb_t_kernel(tc, z, mlp_out, t2, A, W, h, out):
    nc = tc.nc
    with ExitStack() as ctx:
        ctx.enter_context(tc.manual_schedule())
        keep = ctx.enter_context(tc.tile_pool(name="keep", bufs=1))
        stage = ctx.enter_context(tc.tile_pool(name="stage", bufs=2))
        zstage = ctx.enter_context(tc.tile_pool(name="zstage", bufs=6))
        fields = ctx.enter_context(tc.tile_pool(name="fields", bufs=FIELD_BUFS))
        outs = ctx.enter_context(tc.tile_pool(name="outs", bufs=6))
        psum = ctx.enter_context(tc.psum_pool(name="psum", bufs=1))
        bank_uses = []

        def bank(shape, dtype):
            n = len(bank_uses)
            bank_uses.append(n)
            return psum.tile(shape, dtype, tag="bank%d" % (n % BANKS), name="use%d" % n)

        z_raw = keep.tile([P, 5, B], BF16, name="z_raw")
        zq = keep.tile([P, B], U32, name="zq", align_bytes=64)
        zs = keep.tile([P, B], U8, name="zs", align_bytes=64)
        w_raw = keep.tile([P, E * MT, M], BF16, name="w_raw")
        wq = keep.tile([P, E, M], U32, name="wq", align_bytes=64)
        ws = keep.tile([P, E, M], U8, name="ws", align_bytes=64)
        gate_rows = keep.tile([P, B], BF16, name="gate_rows")
        gate_pad = keep.tile([P, NT, P], BF16, name="gate_pad")
        a_pad = keep.tile([P, M], BF16, name="a_pad")
        h_pad = keep.tile([P, M], BF16, name="h_pad")
        h_bc = keep.tile([P, E, M], BF16, name="h_bc")
        dh = keep.tile([P, E - 1, M], F32, name="dh")
        h_col = keep.tile([P, MT], F32, name="h_col")
        ident_f = keep.tile([P, P], F32, name="ident_f")
        ident_b = keep.tile([P, P], BF16, name="ident_b")
        warm = keep.tile([P, 1], F32, name="warm")
        ml_rows = keep.tile([P, P * E], BF16, name="ml_rows")
        t2b = keep.tile([P, 1], BF16, name="t2b")
        t2f = keep.tile([P, 1], F32, name="t2f")
        rinv = keep.tile([P, 1], F32, name="rinv")
        lg = keep.tile([P, NT, E], F32, name="lg")
        mx = keep.tile([P, NT], F32, name="mx")
        ex = keep.tile([P, NT, E], F32, name="ex")
        sm = keep.tile([P, NT], F32, name="sm")
        rs = keep.tile([P, NT], F32, name="rs")
        gate = keep.tile([P, NT, E], F32, name="gate")
        g3m1 = keep.tile([P, NT], F32, name="g3m1")

        z_view = z.rearrange("(t p) b -> p t b", p=P)

        def load_z(g):
            gs = slice(GW * g, GW * (g + 1))
            nc.sync.dma_start(out=z_raw[:, 0, gs], in_=z_view[:, 3, gs])
            nc.sync.dma_start(out=z_raw[:, 1:5, gs], in_=z_view[:, :, gs])

        nc.scalar.dma_start(out=ml_rows[0:NT, :], in_=mlp_out.rearrange("(t p) e -> t (p e)", p=P))
        with nc.allow_non_contiguous_dma(reason="one value to every partition"):
            nc.scalar.dma_start(out=t2b[:], in_=t2.partition_broadcast(P))
        for e in range(E):
            nc.sync.dma_start(
                out=w_raw[:, MT * e:MT * (e + 1), :],
                in_=W[e].rearrange("(mt p) k -> p mt k", p=P),
            )
        load_z(0)
        load_z(1)
        nc.sync.dma_start(out=h_bc[:].rearrange("p e m -> p (e m)"),
                          in_=h.rearrange("e m -> (e m)").partition_broadcast(P))
        for g in range(2, NG):
            load_z(g)

        nc.vector.memset(ml_rows[32:64, :].bitcast(I32), 0)
        nc.vector.memset(ml_rows[64:128, :].bitcast(I32), 0)
        nc.vector.memset(warm[:], 0.0)
        nc.scalar.activation(out=warm[:], in_=warm[:], func=ACT.Exp)
        nc.vector.memset(a_pad[:].bitcast(I32), 0)
        nc.vector.memset(h_pad[:].bitcast(I32), 0)
        nc.vector.memset(gate_pad[:].rearrange("p t c -> p (t c)").bitcast(I32), 0)
        make_identity(nc, ident_b[:])
        make_identity(nc, ident_f[:])
        for part in range(2):
            nc.scalar.dma_start(out=a_pad[E * part:E * (part + 1), :], in_=A)
            nc.scalar.dma_start(out=h_pad[E * part:E * part + 3, :], in_=h[0:3, :])
            nc.scalar.dma_start(out=h_pad[8 + part:9 + part, :], in_=h[3:4, :])

        z_grouped = {}

        def relu_z(g):
            gs = slice(GW * g, GW * (g + 1))
            nc.scalar.activation(out=z_raw[96:128, 0, gs], in_=z_raw[96:128, 0, gs], func=ACT.Relu)

        def regroup_z(tb):
            cs = slice(P * tb, P * (tb + 1))
            zg = zstage.tile([P, P, 4], BF16, tag="zg", align_bytes=64)
            nc.scalar.copy(
                out=zg[:].rearrange("p (c i) t -> p c t i", i=4),
                in_=z_raw[:, 0:4, cs].rearrange("p t (c i) -> p c t i", i=4),
            )
            z_grouped[tb] = zg

        def quantise_z(tb):
            cs = slice(P * tb, P * (tb + 1))
            nc.vector.quantize_mx(out=zq[:, cs].bitcast(FP8X4), scales=zs[:, cs],
                                  in_=z_grouped[tb][:].rearrange("p b t -> p (b t)"))

        def softmax_first():
            nc.vector.tensor_copy(out=t2f[:], in_=t2b[:])
            nc.vector.reciprocal(out=rinv[:], in_=t2f[:])
            nc.vector.tensor_scalar(out=lg[:], in0=ml_cols[:, :, 0:NT].rearrange("p e t -> p t e"),
                                    scalar1=rinv[:, 0:1], scalar2=-1.0, op0=ALU.mult, op1=ALU.mult)
            nc.vector.tensor_reduce(out=mx[:], in_=lg[:], axis=AX.X, op=ALU.max)
            nc.vector.tensor_tensor(out=lg[:], in0=lg[:], in1=mx[:].unsqueeze(2).to_broadcast([P, NT, E]),
                                    op=ALU.subtract)
            nc.scalar.activation(out=ex[:], in_=lg[:], func=ACT.Exp)

        def softmax_second():
            nc.vector.tensor_reduce(out=sm[:], in_=ex[:], axis=AX.X, op=ALU.add)
            nc.vector.reciprocal(out=rs[:], in_=sm[:])
            nc.vector.tensor_tensor(out=gate[:], in0=ex[:], in1=rs[:].unsqueeze(2).to_broadcast([P, NT, E]),
                                    op=ALU.mult)

        def gate_parts():
            nc.vector.tensor_copy(out=gate_pad[:, :, 0:E], in_=gate[:])
            nc.vector.tensor_tensor(out=gate_pad[:, :, E:2 * E], in0=gate[:], in1=gate_pad[:, :, 0:E],
                                    op=ALU.subtract)
            nc.vector.tensor_scalar_add(out=g3m1[:], in0=gate[:, :, 3], scalar1=-1.0)
            nc.vector.tensor_copy(out=gate_pad[:, :, 8], in_=g3m1[:])
            nc.vector.tensor_tensor(out=gate_pad[:, :, 9], in0=g3m1[:], in1=gate_pad[:, :, 8], op=ALU.subtract)

        ml_cols = bank([P, E, P], BF16)
        for e in range(E):
            nc.tensor.transpose(ml_cols[:, e, :], ml_rows[:].rearrange("t (p e) -> t e p", e=E)[:, e, :], ident_b[:])

        w_banks = {}
        w_grouped = {}
        for e in range(E):
            w_grouped[e] = keep.tile([P, M, 4], BF16, name="wg%d" % e, align_bytes=64)
            for half in range(2):
                xt = bank([P, 8, P], BF16)
                for a in range(2):
                    mt = 2 * half + a
                    for j in range(4):
                        t = (j + 3) % 4
                        nc.tensor.transpose(xt[:, 4 * a + j, :], w_raw[:, MT * e + mt, P * t:P * (t + 1)],
                                            ident_b[:])
                w_banks[(e, half)] = xt

        def w_exit(e, half, on_vector):
            dst = w_grouped[e][:, 256 * half:256 * (half + 1), :].rearrange("p (a r) j -> p a r j", a=2)
            src = w_banks[(e, half)][:].rearrange("p (a j) r -> p a r j", a=2)
            if on_vector:
                nc.vector.tensor_copy(out=dst, in_=src)
            else:
                nc.scalar.copy(out=dst, in_=src)

        def w_quantise(e):
            nc.vector.quantize_mx(out=wq[:, e, :].bitcast(FP8X4), scales=ws[:, e, :],
                                  in_=w_grouped[e][:].rearrange("p m j -> p (m j)"))

        w_exit(0, 1, True)
        w_exit(0, 0, False)
        w_exit(1, 0, True)
        w_exit(1, 1, False)
        w_quantise(0)
        w_exit(2, 1, False)
        softmax_first()
        w_exit(2, 0, True)
        relu_z(0)
        w_quantise(1)
        regroup_z(0)
        w_quantise(2)
        regroup_z(1)
        softmax_second()
        w_exit(3, 0, False)
        quantise_z(0)
        regroup_z(2)
        w_exit(3, 1, True)
        quantise_z(1)
        w_quantise(3)

        def gate_quarter(q):
            wt = bank([P, 8, P], BF16)
            for i in range(8):
                nc.tensor.transpose(wt[:, i, :], gate_pad[:, 8 * q + i, :], ident_b[:])
            nc.vector.tensor_copy(out=gate_rows[:, 1024 * q:1024 * (q + 1)],
                                  in_=wt[:].rearrange("p t c -> p (t c)"))

        def h3_column():
            ht = bank([P, MT, P], BF16)
            for mt in range(MT):
                nc.tensor.transpose(ht[:, mt, :], h_pad[:, P * mt:P * (mt + 1)], ident_b[:])
            nc.vector.tensor_copy(out=h_col[:], in_=ht[:, :, 8])

        for e in range(E - 1):
            nc.gpsimd.tensor_tensor(out=dh[:, e, :], in0=h_bc[:, e, :], in1=h_bc[:, 3, :], op=ALU.subtract)
        off_tiles = [TPG * g + i for g in range(NG) for i in range(TPG - OFF_TILES[g], TPG)]
        product_fields = {}
        for tb in off_tiles:
            gh = keep.tile([P, M], F32, name="gh%d" % tb)
            nc.gpsimd.tensor_scalar(out=gh[:], in0=dh[:, 0, :], scalar1=gate[:, tb, 0:1], scalar2=0.0,
                                    op0=ALU.mult, op1=ALU.add)
            for e in range(1, E - 1):
                tm = stage.tile([P, M], F32, tag="tm")
                nc.gpsimd.tensor_scalar(out=tm[:], in0=dh[:, e, :], scalar1=gate[:, tb, e:e + 1], scalar2=0.0,
                                        op0=ALU.mult, op1=ALU.add)
                nc.gpsimd.tensor_tensor(out=gh[:], in0=gh[:], in1=tm[:], op=ALU.add)
            product_fields[tb] = [gh]

        banks = {}
        tile_fields = {}
        unit_banks = {}
        unit_out = {}

        def mx_pass(tb, e):
            bs = slice(P * tb, P * (tb + 1))
            pe = bank([P, M], F32)
            nc.tensor.matmul_mx(out=pe[:], lhsT=zq[:, bs].bitcast(FP8X4), lhsT_scale=zs[:, bs],
                                rhs=wq[:, e, :].bitcast(FP8X4), rhs_scale=ws[:, e, :],
                                start=True, stop=True)
            banks[(tb, e)] = pe

        def scalar_exit(tb, e):
            fld = fields.tile([P, M], F32, tag="f%d" % (e // 2))
            nc.scalar.activation(out=fld[:], in_=banks[(tb, e)][:], func=ACT.Copy, scale=gate[:, tb, e:e + 1])
            tile_fields[tb] = tile_fields.get(tb, []) + [fld]

        def vector_exit(tb, e):
            fld = tile_fields[tb][e // 2]
            nc.vector.scalar_tensor_tensor(out=fld[:], in0=banks[(tb, e)][:], scalar=gate[:, tb, e:e + 1],
                                           in1=fld[:], op0=ALU.mult, op1=ALU.add)

        def plain_part(u):
            g, mt = u // MT, u % MT
            gs = slice(GW * g, GW * (g + 1))
            ms = slice(P * mt, P * (mt + 1))
            wide = GW - P * OFF_TILES[g]
            todo = [(i, fld) for i in range(TPG)
                    for fld in tile_fields[TPG * g + i] + product_fields.get(TPG * g + i, [])]
            b2 = bank([P, GW], F32)
            nc.tensor.matmul(out=b2[:], lhsT=a_pad[:, ms], rhs=gate_rows[:, gs], start=True, stop=True)
            b1 = bank([P, GW], F32)
            nc.tensor.matmul(out=b1[:, 0:wide], lhsT=h_pad[:, ms],
                             rhs=gate_rows[:, GW * g:GW * g + wide], start=True, stop=False)
            for n, (i, fld) in enumerate(todo):
                nc.tensor.matmul(out=b1[:, P * i:P * (i + 1)], lhsT=fld[:, ms], rhs=ident_f[:],
                                 is_transpose=True, start=False, stop=(n == len(todo) - 1))
            unit_banks[u] = (b2, b1)

        def times_z(u):
            g, mt = u // MT, u % MT
            xs = outs.tile([P, GW], F32, tag="xs")
            nc.vector.tensor_tensor(out=xs[:], in0=unit_banks[u][0][:],
                                    in1=z_raw[:, 1 + mt, GW * g:GW * (g + 1)], op=ALU.mult)
            unit_out[u] = xs

        def last_add(u):
            g, mt = u // MT, u % MT
            xs = unit_out[u]
            nc.vector.scalar_tensor_tensor(out=xs[:], in0=unit_banks[u][1][:], scalar=h_col[:, mt:mt + 1],
                                           in1=xs[:], op0=ALU.add, op1=ALU.add)
            nc.sync.dma_start(out=out[P * mt:P * (mt + 1), GW * g:GW * (g + 1)], in_=xs[:])

        UNITS = NG * MT
        for s in range(-1, NT + LAG + 1):
            u = s - LAG
            for e_scalar, e_vector in ((0, 1), (2, 3)):
                if s + 1 < NT:
                    mx_pass(s + 1, e_scalar)
                if 0 <= s < NT:
                    mx_pass(s, e_vector)
            if 0 <= u < UNITS:
                plain_part(u)
            if s + 1 < NT:
                scalar_exit(s + 1, 0)
                scalar_exit(s + 1, 2)
            nxt = s + AHEAD_COPY
            if nxt < NT:
                if nxt % TPG == 0:
                    relu_z(nxt // TPG)
                regroup_z(nxt)
            if 0 <= u - 1 < UNITS:
                last_add(u - 1)
            if 0 <= s < NT:
                vector_exit(s, 1)
                vector_exit(s, 3)
            if 0 <= u < UNITS:
                times_z(u)
            if s == -1:
                gate_parts()
            if s == 0:
                gate_quarter(0)
                h3_column()
            if 1 <= s <= 3:
                gate_quarter(s)
            if s + AHEAD_QUANT < NT:
                quantise_z(s + AHEAD_QUANT)
